import numpy as np
import ml_dtypes


def mxq(x, axis, fmt="e4m3"):
    dtype, down = {"e4m3": (ml_dtypes.float8_e4m3fn, 7), "e5m2": (ml_dtypes.float8_e5m2, 14)}[fmt]
    v = np.moveaxis(np.asarray(x, np.float32).astype(ml_dtypes.bfloat16).astype(np.float64), axis, -1)
    blocks = v.reshape(v.shape[:-1] + (-1, 32))
    amax = np.abs(blocks).max(-1, keepdims=True)
    byte = np.maximum(np.where(amax > 0, np.frexp(amax)[1] - 1 + 127, 0) - down, 1)
    scale = np.exp2(byte - 127.0)
    codes = (blocks / scale).astype(np.float32).astype(dtype).astype(np.float64)
    return np.moveaxis((codes * scale).reshape(v.shape), -1, axis)


WIDE = False


def mx_kscale(k):
    if not WIDE:
        return np.ones(k)
    levels = np.array([10, -10, 5, -5, 0])
    a = np.random.permutation(np.resize(levels, k // 512 * 4)).reshape(k // 512, 4)
    idx = np.arange(k)
    return np.exp2(a[idx // 512, idx % 128 // 32])


BF16 = ml_dtypes.bfloat16


def bf(x):
    return np.asarray(x, np.float32).astype(BF16)


def f64(x):
    return np.asarray(x).astype(np.float64)


E2M1 = np.array([0.0, 0.5, 1.0, 1.5, 2.0, 3.0, 4.0, 6.0, -0.0, -0.5, -1.0, -1.5, -2.0, -3.0, -4.0, -6.0])


def pack_weight(w, fmt):
    k, n = w.shape
    w = f64(bf(w)).reshape(k // 32, 32, n)
    amax = np.abs(w).max(1)
    if fmt == "e4m3":
        byte = np.frexp(amax)[1] - 1 + 127 - 7
    else:
        mant, ex = np.frexp(amax / 6.0)
        byte = np.where(mant > 0.5, ex, ex - 1) + 127
    byte = np.clip(np.where(amax > 0, byte, 1), 1, 254)
    scaled = (w * np.exp2(127.0 - byte)[:, None, :]).reshape(k, n).astype(np.float32)
    by_word = np.ascontiguousarray(scaled.reshape(k // 512, 128, 4, n).transpose(0, 1, 3, 2))
    if fmt == "e4m3":
        words = by_word.astype(ml_dtypes.float8_e4m3fn).view(np.uint8)
    else:
        c = by_word.astype(ml_dtypes.float4_e2m1fn).view(np.uint8) & 0xF
        words = c[..., 0::2] | (c[..., 1::2] << 4)
    return np.ascontiguousarray(words), np.ascontiguousarray(byte.astype(np.uint8).reshape(k // 512, 16, n))


def unpack_weight(words, scales, fmt):
    g, p, n, _ = words.shape
    if fmt == "e4m3":
        vals = np.ascontiguousarray(words).view(ml_dtypes.float8_e4m3fn).astype(np.float64)
    else:
        nib = np.empty((g, p, n, 4), np.uint8)
        nib[..., 0::2] = words & 0xF
        nib[..., 1::2] = words >> 4
        vals = E2M1[nib]
    vals = vals * np.repeat(np.exp2(scales.astype(np.float64) - 127.0), 8, axis=1)[..., None]
    return vals.transpose(0, 1, 3, 2).reshape(g * 512, n)


B, S, E, H, KV, DH = 1, 512, 2048, 16, 4, 128
THETA = 10000.0
FMT = "e4m3"


def rope(x):
    b, s, h, hd = x.shape
    half = hd // 2
    inv_freq = 1.0 / THETA ** (f64(np.arange(0, half, 2)) / half)
    pos = np.broadcast_to(f64(np.arange(s))[None, :], (b, s))
    freqs = pos[:, :, None] * inv_freq[None, None, :]
    cos = np.cos(freqs)[:, :, None, :]
    sin = np.sin(freqs)[:, :, None, :]
    pairs = x[..., :half].reshape(b, s, h, half // 2, 2)
    x0, x1 = pairs[..., 0], pairs[..., 1]
    rot = np.stack([x0 * cos - x1 * sin, x0 * sin + x1 * cos], axis=-1).reshape(b, s, h, half)
    return np.concatenate([rot, x[..., half:]], axis=-1)


def setup_inputs():
    s = mx_kscale(E)
    hidden_states = bf(np.random.standard_normal((B, S, E)) * s)
    wq_words, wq_scales = pack_weight(np.random.standard_normal((E, H * DH)) * 1.25 / np.sqrt(E) / s[:, None], FMT)
    wk_words, wk_scales = pack_weight(np.random.standard_normal((E, KV * DH)) * 1.25 / np.sqrt(E) / s[:, None], FMT)
    wv_words, wv_scales = pack_weight(np.random.standard_normal((E, KV * DH)) * 1.25 / np.sqrt(E) / s[:, None], FMT)
    return {"hidden_states": hidden_states,
            "Wq_words": wq_words, "Wq_scales": wq_scales,
            "Wk_words": wk_words, "Wk_scales": wk_scales,
            "Wv_words": wv_words, "Wv_scales": wv_scales}


def reference(hidden_states, Wq_words, Wq_scales, Wk_words, Wk_scales, Wv_words, Wv_scales):
    xq = mxq(f64(hidden_states), 2, "e4m3")
    q = (xq @ unpack_weight(Wq_words, Wq_scales, FMT)).reshape(B, S, H, DH)
    k = (xq @ unpack_weight(Wk_words, Wk_scales, FMT)).reshape(B, S, KV, DH)
    v = (xq @ unpack_weight(Wv_words, Wv_scales, FMT)).reshape(B, S, KV, DH)
    return rope(q), rope(k), v

@@ -1,0 +1,206 @@
+import math
+from contextlib import ExitStack
+
+import concourse.mybir as mybir
+from concourse.masks import make_identity
+
+F32 = mybir.dt.float32
+BF16 = mybir.dt.bfloat16
+I32 = mybir.dt.int32
+U32 = mybir.dt.uint32
+U8 = mybir.dt.uint8
+FP8X4 = mybir.dt.float8_e4m3fn_x4
+ALU = mybir.AluOpType
+ACT = mybir.ActivationFunctionType
+
+P = 128
+TOKENS = 512
+K = 2048
+K_PASS = 512
+PASSES = K // K_PASS
+TOKEN_TILES = TOKENS // P
+CHUNK = 512
+HEAD = 128
+HEADS_IN_CHUNK = CHUNK // HEAD
+ROTATED = 64
+PAIRS = ROTATED // 2
+Q_FEATURES = 2048
+KV_FEATURES = 512
+FEATURES = Q_FEATURES + 2 * KV_FEATURES
+
+THETA = 10000.0
+FREQ_RATIO = THETA ** (-1.0 / PAIRS)
+
+ROUND_MAGIC = 12582912.0
+TWO_PI = 2.0 * math.pi
+TWO_PI_HIGH = 6.28125
+TWO_PI_MID = math.floor((TWO_PI - TWO_PI_HIGH) * 2.0**26) / 2.0**26
+TWO_PI_LOW = TWO_PI - TWO_PI_HIGH - TWO_PI_MID
+
+NEG_SIN = 0
+SIN = 1
+COS = 2
+
+FLOPS = 2 * TOKENS * K * FEATURES
+
+
+def tile_diffucoderattention_pa_kernel(
+    tc, hidden_states, Wq_words, Wq_scales, Wk_words, Wk_scales, Wv_words, Wv_scales, out_0, out_1, out_2
+):
+    nc = tc.nc
+    x = hidden_states.flatten_outer_dims()
+
+    def words_by_partition(words):
+        return words.rearrange("g p n t -> p g (n t)").bitcast(I32)
+
+    def rows_by_token(out):
+        return out.rearrange("b s h d -> (b s) (h d)")
+
+    chunks = []
+    for c in range(Q_FEATURES // CHUNK):
+        cols = slice(c * CHUNK, (c + 1) * CHUNK)
+        chunks.append((words_by_partition(Wq_words)[:, :, cols], rows_by_token(out_0)[:, cols], True))
+    chunks.append((words_by_partition(Wk_words), rows_by_token(out_1), True))
+    chunks.append((words_by_partition(Wv_words), rows_by_token(out_2), False))
+
+    with ExitStack() as ctx:
+        keep = ctx.enter_context(tc.tile_pool(name="keep", bufs=1))
+        cross_pool = ctx.enter_context(tc.tile_pool(name="cross", bufs=3))
+        y_pool = ctx.enter_context(tc.tile_pool(name="y", bufs=len(chunks) * TOKEN_TILES))
+        psum = ctx.enter_context(tc.psum_pool(name="psum", bufs=8))
+
+        w_scales = keep.tile([P, FEATURES], U8, align_bytes=64)
+        nc.vector.memset(w_scales[:].bitcast(I32), 0)
+        first_col = 0
+        for scales in (Wq_scales, Wk_scales, Wv_scales):
+            n = scales.shape[2]
+            for quad in range(4):
+                nc.scalar.dma_start(
+                    out=w_scales[32 * quad : 32 * quad + 16, first_col : first_col + n].bitcast(F32),
+                    in_=scales[:, 4 * quad : 4 * quad + 4, :].bitcast(F32),
+                )
+            first_col += n
+
+        x_sb = keep.tile([P, TOKEN_TILES, K], BF16)
+        for t in range(TOKEN_TILES):
+            nc.sync.dma_start(out=x_sb[:, t, :], in_=x[t * P : (t + 1) * P, :])
+
+        w_words = []
+        for c in range(len(chunks)):
+            w = keep.tile([P, PASSES, CHUNK], U32, name="w%d" % c, align_bytes=64)
+            nc.sync.dma_start(out=w[:].bitcast(I32), in_=chunks[c][0])
+            w_words.append(w)
+
+        position_int = keep.tile([P, TOKEN_TILES], I32)
+        nc.gpsimd.iota(position_int[:], pattern=[[P, TOKEN_TILES]], base=0, channel_multiplier=1)
+        identity = keep.tile([P, P], F32)
+        make_identity(nc, identity[:])
+
+        position = keep.tile([P, TOKEN_TILES], F32)
+        nc.vector.tensor_copy(out=position[:], in_=position_int[:])
+        freq = keep.tile([P, PAIRS], F32)
+        nc.vector.memset(freq[:, 0:1], 1.0)
+        for doubling in range(5):
+            width = 2**doubling
+            nc.vector.tensor_scalar(
+                out=freq[:, width : 2 * width],
+                in0=freq[:, 0:width],
+                scalar1=FREQ_RATIO**width,
+                scalar2=None,
+                op0=ALU.mult,
+            )
+        table_shape = [P, TOKEN_TILES, PAIRS]
+        phase = keep.tile([P, 3, TOKEN_TILES, PAIRS], F32)
+        nc.vector.tensor_tensor(
+            out=phase[:, SIN],
+            in0=position[:].unsqueeze(2).to_broadcast(table_shape),
+            in1=freq[:].unsqueeze(1).to_broadcast(table_shape),
+            op=ALU.mult,
+        )
+        nc.vector.tensor_scalar(out=phase[:, NEG_SIN], in0=phase[:, SIN], scalar1=-1.0, scalar2=None, op0=ALU.mult)
+        nc.vector.tensor_scalar(
+            out=phase[:, COS], in0=phase[:, SIN], scalar1=math.pi / 2.0, scalar2=None, op0=ALU.add
+        )
+        turns = keep.tile([P, 3, TOKEN_TILES, PAIRS], F32)
+        nc.vector.tensor_scalar(
+            out=turns[:], in0=phase[:], scalar1=1.0 / TWO_PI, scalar2=ROUND_MAGIC, op0=ALU.mult, op1=ALU.add
+        )
+        nc.vector.tensor_scalar(out=turns[:], in0=turns[:], scalar1=ROUND_MAGIC, scalar2=None, op0=ALU.subtract)
+        for part in (TWO_PI_HIGH, TWO_PI_MID, TWO_PI_LOW):
+            nc.vector.scalar_tensor_tensor(
+                out=phase[:], in0=turns[:], scalar=-part, in1=phase[:], op0=ALU.mult, op1=ALU.add
+            )
+        trig = keep.tile([P, 3, TOKEN_TILES, PAIRS], F32)
+        nc.scalar.activation(out=trig[:], in_=phase[:], func=ACT.Sin)
+
+        grouped = keep.tile([P, TOKEN_TILES, PASSES * P * 4], BF16, align_bytes=64)
+        x_codes = keep.tile([P, TOKEN_TILES, PASSES * P], U32, align_bytes=64)
+        x_scales = keep.tile([P, TOKEN_TILES, PASSES * P], U8, align_bytes=64)
+        for t in range(TOKEN_TILES):
+            x_as_words = x_sb[:, t, :].bitcast(F32)
+            grouped_as_words = grouped[:, t, :].bitcast(F32)
+            for half in range(2):
+                flipped = psum.tile([P, 2, 2, P], F32, tag="bank")
+                for g2 in range(2):
+                    g = 2 * half + g2
+                    for u in range(2):
+                        nc.tensor.transpose(
+                            flipped[:, g2, u, :], x_as_words[:, 256 * g + u : 256 * (g + 1) : 2], identity[:]
+                        )
+                side_by_side = grouped_as_words[:, 512 * half : 512 * (half + 1)].rearrange(
+                    "p (g r u) -> p g r u", g=2, u=2
+                )
+                if half == 0:
+                    nc.vector.tensor_copy(out=side_by_side, in_=flipped[:].rearrange("p g u r -> p g r u"))
+                else:
+                    nc.scalar.copy(out=side_by_side, in_=flipped[:].rearrange("p g u r -> p g r u"))
+            nc.vector.quantize_mx(out=x_codes[:, t, :].bitcast(FP8X4), scales=x_scales[:, t, :], in_=grouped[:, t, :])
+
+        for c in range(len(chunks)):
+            out_rows = chunks[c][1]
+            rotated = chunks[c][2]
+            for t in range(TOKEN_TILES):
+                acc = psum.tile([P, CHUNK], F32, tag="bank")
+                for g in range(PASSES):
+                    nc.tensor.matmul_mx(
+                        out=acc[:],
+                        lhsT=x_codes[:, t, g * P : (g + 1) * P].bitcast(FP8X4),
+                        lhsT_scale=x_scales[:, t, g * P : (g + 1) * P],
+                        rhs=w_words[c][:, g, :].bitcast(FP8X4),
+                        rhs_scale=w_scales[4 * g : P, c * CHUNK : (c + 1) * CHUNK],
+                        start=(g == 0),
+                        stop=(g == PASSES - 1),
+                    )
+                y = y_pool.tile([P, CHUNK], F32, tag="y")
+                if rotated:
+                    acc_heads = acc[:].rearrange("p (h d) -> p h d", d=HEAD)
+                    y_heads = y[:].rearrange("p (h d) -> p h d", d=HEAD)
+                    nc.scalar.copy(out=y_heads[:, :, ROTATED:], in_=acc_heads[:, :, ROTATED:])
+                    acc_pairs = acc_heads[:, :, :ROTATED].rearrange("p h (i e) -> p h i e", e=2)
+                    y_pairs = y_heads[:, :, :ROTATED].rearrange("p h (i e) -> p h i e", e=2)
+                    plane_shape = [P, HEADS_IN_CHUNK, PAIRS]
+                    nc.vector.tensor_tensor(
+                        out=y_pairs,
+                        in0=acc_pairs,
+                        in1=trig[:, COS, t, :].unsqueeze(1).unsqueeze(3).to_broadcast(plane_shape + [2]),
+                        op=ALU.mult,
+                    )
+                    cross = cross_pool.tile([P, 2, HEADS_IN_CHUNK, PAIRS], F32)
+                    nc.vector.tensor_tensor(
+                        out=cross[:, 0],
+                        in0=acc_pairs[:, :, :, 1],
+                        in1=trig[:, NEG_SIN, t, :].unsqueeze(1).to_broadcast(plane_shape),
+                        op=ALU.mult,
+                    )
+                    nc.vector.tensor_tensor(
+                        out=cross[:, 1],
+                        in0=acc_pairs[:, :, :, 0],
+                        in1=trig[:, SIN, t, :].unsqueeze(1).to_broadcast(plane_shape),
+                        op=ALU.mult,
+                    )
+                    nc.vector.tensor_tensor(
+                        out=y_pairs, in0=y_pairs, in1=cross[:].rearrange("p e h i -> p h i e"), op=ALU.add
+                    )
+                else:
+                    nc.scalar.copy(out=y[:], in_=acc[:])
+                nc.sync.dma_start(out=out_rows[t * P : (t + 1) * P, :], in_=y[:])

@@ -18,6 +18,7 @@ TOKENS = 512
 K = 2048
 K_PASS = 512
 PASSES = K // K_PASS
+HALF_PASSES = PASSES // 2
 TOKEN_TILES = TOKENS // P
 CHUNK = 512
 HEAD = 128
@@ -59,36 +60,46 @@ def tile_diffucoderattention_pa_kernel(
     chunks = []
     for c in range(Q_FEATURES // CHUNK):
         cols = slice(c * CHUNK, (c + 1) * CHUNK)
-        chunks.append((words_by_partition(Wq_words)[:, :, cols], rows_by_token(out_0)[:, cols], True))
-    chunks.append((words_by_partition(Wk_words), rows_by_token(out_1), True))
-    chunks.append((words_by_partition(Wv_words), rows_by_token(out_2), False))
+        chunks.append(
+            (words_by_partition(Wq_words)[:, :, cols], rows_by_token(out_0)[:, cols], True, Wq_scales if c == 0 else None)
+        )
+    chunks.append((words_by_partition(Wk_words), rows_by_token(out_1), True, Wk_scales))
+    chunks.append((words_by_partition(Wv_words), rows_by_token(out_2), False, Wv_scales))
+
+    def pass_rounds(c):
+        if c == 0:
+            return (slice(0, HALF_PASSES), slice(HALF_PASSES, PASSES))
+        return (slice(0, PASSES),)
 
     with ExitStack() as ctx:
         keep = ctx.enter_context(tc.tile_pool(name="keep", bufs=1))
         cross_pool = ctx.enter_context(tc.tile_pool(name="cross", bufs=3))
         y_pool = ctx.enter_context(tc.tile_pool(name="y", bufs=len(chunks) * TOKEN_TILES))
         psum = ctx.enter_context(tc.psum_pool(name="psum", bufs=8))
-
-        w_scales = keep.tile([P, FEATURES], U8, align_bytes=64)
-        nc.vector.memset(w_scales[:].bitcast(I32), 0)
-        first_col = 0
-        for scales in (Wq_scales, Wk_scales, Wv_scales):
-            n = scales.shape[2]
-            for quad in range(4):
-                nc.scalar.dma_start(
-                    out=w_scales[32 * quad : 32 * quad + 16, first_col : first_col + n].bitcast(F32),
-                    in_=scales[:, 4 * quad : 4 * quad + 4, :].bitcast(F32),
-                )
-            first_col += n
+        ctx.enter_context(tc.manual_schedule())
 
         x_sb = keep.tile([P, TOKEN_TILES, K], BF16)
         for t in range(TOKEN_TILES):
             nc.sync.dma_start(out=x_sb[:, t, :], in_=x[t * P : (t + 1) * P, :])
 
+        w_scales = keep.tile([P, FEATURES], U8, align_bytes=64)
+        nc.vector.memset(w_scales[:].bitcast(I32), 0)
+
+        def load_scales(scales, first_col):
+            cols = slice(first_col, first_col + scales.shape[2])
+            for quad in range(4):
+                nc.sync.dma_start(
+                    out=w_scales[32 * quad : 32 * quad + 16, cols].bitcast(I32),
+                    in_=scales[:, 4 * quad : 4 * quad + 4, :].bitcast(I32),
+                )
+
         w_words = []
         for c in range(len(chunks)):
+            if chunks[c][3] is not None:
+                load_scales(chunks[c][3], c * CHUNK)
             w = keep.tile([P, PASSES, CHUNK], U32, name="w%d" % c, align_bytes=64)
-            nc.sync.dma_start(out=w[:].bitcast(I32), in_=chunks[c][0])
+            for some in pass_rounds(c):
+                nc.sync.dma_start(out=w[:, some, :].bitcast(I32), in_=chunks[c][0][:, some, :])
             w_words.append(w)
 
         position_int = keep.tile([P, TOKEN_TILES], I32)
@@ -96,10 +107,10 @@ def tile_diffucoderattention_pa_kernel(
         identity = keep.tile([P, P], F32)
         make_identity(nc, identity[:])
 
-        position = keep.tile([P, TOKEN_TILES], F32)
-        nc.vector.tensor_copy(out=position[:], in_=position_int[:])
         freq = keep.tile([P, PAIRS], F32)
         nc.vector.memset(freq[:, 0:1], 1.0)
+        early_sin = keep.tile([P, 1], F32)
+        nc.scalar.activation(out=early_sin[:], in_=freq[:, 0:1], func=ACT.Sin)
         for doubling in range(5):
             width = 2**doubling
             nc.vector.tensor_scalar(
@@ -109,6 +120,8 @@ def tile_diffucoderattention_pa_kernel(
                 scalar2=None,
                 op0=ALU.mult,
             )
+        position = keep.tile([P, TOKEN_TILES], F32)
+        nc.vector.tensor_copy(out=position[:], in_=position_int[:])
         table_shape = [P, TOKEN_TILES, PAIRS]
         phase = keep.tile([P, 3, TOKEN_TILES, PAIRS], F32)
         nc.vector.tensor_tensor(
@@ -136,6 +149,10 @@ def tile_diffucoderattention_pa_kernel(
         grouped = keep.tile([P, TOKEN_TILES, PASSES * P * 4], BF16, align_bytes=64)
         x_codes = keep.tile([P, TOKEN_TILES, PASSES * P], U32, align_bytes=64)
         x_scales = keep.tile([P, TOKEN_TILES, PASSES * P], U8, align_bytes=64)
+
+        def quantise(t):
+            nc.vector.quantize_mx(out=x_codes[:, t, :].bitcast(FP8X4), scales=x_scales[:, t, :], in_=grouped[:, t, :])
+
         for t in range(TOKEN_TILES):
             x_as_words = x_sb[:, t, :].bitcast(F32)
             grouped_as_words = grouped[:, t, :].bitcast(F32)
@@ -154,23 +171,31 @@ def tile_diffucoderattention_pa_kernel(
                     nc.vector.tensor_copy(out=side_by_side, in_=flipped[:].rearrange("p g u r -> p g r u"))
                 else:
                     nc.scalar.copy(out=side_by_side, in_=flipped[:].rearrange("p g u r -> p g r u"))
-            nc.vector.quantize_mx(out=x_codes[:, t, :].bitcast(FP8X4), scales=x_scales[:, t, :], in_=grouped[:, t, :])
+            if t > 0:
+                quantise(t - 1)
+        quantise(TOKEN_TILES - 1)
 
         for c in range(len(chunks)):
             out_rows = chunks[c][1]
             rotated = chunks[c][2]
+            accs = []
             for t in range(TOKEN_TILES):
                 acc = psum.tile([P, CHUNK], F32, tag="bank")
-                for g in range(PASSES):
-                    nc.tensor.matmul_mx(
-                        out=acc[:],
-                        lhsT=x_codes[:, t, g * P : (g + 1) * P].bitcast(FP8X4),
-                        lhsT_scale=x_scales[:, t, g * P : (g + 1) * P],
-                        rhs=w_words[c][:, g, :].bitcast(FP8X4),
-                        rhs_scale=w_scales[4 * g : P, c * CHUNK : (c + 1) * CHUNK],
-                        start=(g == 0),
-                        stop=(g == PASSES - 1),
-                    )
+                accs.append(acc)
+            for some in pass_rounds(c):
+                for t in range(TOKEN_TILES):
+                    for g in range(PASSES)[some]:
+                        nc.tensor.matmul_mx(
+                            out=accs[t][:],
+                            lhsT=x_codes[:, t, g * P : (g + 1) * P].bitcast(FP8X4),
+                            lhsT_scale=x_scales[:, t, g * P : (g + 1) * P],
+                            rhs=w_words[c][:, g, :].bitcast(FP8X4),
+                            rhs_scale=w_scales[4 * g : P, c * CHUNK : (c + 1) * CHUNK],
+                            start=(g == 0),
+                            stop=(g == PASSES - 1),
+                        )
+            for t in range(TOKEN_TILES):
+                acc = accs[t]
                 y = y_pool.tile([P, CHUNK], F32, tag="y")
                 if rotated:
                     acc_heads = acc[:].rearrange("p (h d) -> p h d", d=HEAD)

@@ -57,24 +57,20 @@ def tile_diffucoderattention_pa_kernel(
     def rows_by_token(out):
         return out.rearrange("b s h d -> (b s) (h d)")
 
-    chunks = []
-    for c in range(Q_FEATURES // CHUNK):
-        cols = slice(c * CHUNK, (c + 1) * CHUNK)
-        chunks.append(
-            (words_by_partition(Wq_words)[:, :, cols], rows_by_token(out_0)[:, cols], True, Wq_scales if c == 0 else None)
-        )
-    chunks.append((words_by_partition(Wk_words), rows_by_token(out_1), True, Wk_scales))
-    chunks.append((words_by_partition(Wv_words), rows_by_token(out_2), False, Wv_scales))
-
-    def pass_rounds(c):
-        if c == 0:
-            return (slice(0, HALF_PASSES), slice(HALF_PASSES, PASSES))
-        return (slice(0, PASSES),)
+    q_low = slice(0, Q_FEATURES // 2)
+    q_high = slice(Q_FEATURES // 2, Q_FEATURES)
+    groups = (
+        (words_by_partition(Wq_words)[:, :, q_low], Wq_scales, rows_by_token(out_0)[:, q_low], True),
+        (words_by_partition(Wq_words)[:, :, q_high], None, rows_by_token(out_0)[:, q_high], True),
+        (words_by_partition(Wk_words), Wk_scales, rows_by_token(out_1), True),
+        (words_by_partition(Wv_words), Wv_scales, rows_by_token(out_2), False),
+    )
+    both_rounds = (slice(0, HALF_PASSES), slice(HALF_PASSES, PASSES))
+    one_round = (slice(0, PASSES),)
 
     with ExitStack() as ctx:
         keep = ctx.enter_context(tc.tile_pool(name="keep", bufs=1))
         cross_pool = ctx.enter_context(tc.tile_pool(name="cross", bufs=3))
-        y_pool = ctx.enter_context(tc.tile_pool(name="y", bufs=len(chunks) * TOKEN_TILES))
         psum = ctx.enter_context(tc.psum_pool(name="psum", bufs=8))
         ctx.enter_context(tc.manual_schedule())
 
@@ -85,22 +81,29 @@ def tile_diffucoderattention_pa_kernel(
         w_scales = keep.tile([P, FEATURES], U8, align_bytes=64)
         nc.vector.memset(w_scales[:].bitcast(I32), 0)
 
-        def load_scales(scales, first_col):
-            cols = slice(first_col, first_col + scales.shape[2])
-            for quad in range(4):
-                nc.sync.dma_start(
-                    out=w_scales[32 * quad : 32 * quad + 16, cols].bitcast(I32),
-                    in_=scales[:, 4 * quad : 4 * quad + 4, :].bitcast(I32),
-                )
-
         w_words = []
-        for c in range(len(chunks)):
-            if chunks[c][3] is not None:
-                load_scales(chunks[c][3], c * CHUNK)
-            w = keep.tile([P, PASSES, CHUNK], U32, name="w%d" % c, align_bytes=64)
-            for some in pass_rounds(c):
-                nc.sync.dma_start(out=w[:, some, :].bitcast(I32), in_=chunks[c][0][:, some, :])
+        first_features = []
+        first_feature = 0
+        for words, scales, out_rows, rotated in groups:
+            width = words.shape[2]
+            if scales is not None:
+                for quad in range(4):
+                    nc.sync.dma_start(
+                        out=w_scales[
+                            32 * quad : 32 * quad + 16, first_feature : first_feature + scales.shape[2]
+                        ].bitcast(I32),
+                        in_=scales[:, 4 * quad : 4 * quad + 4, :].bitcast(I32),
+                    )
+            w = keep.tile([P, PASSES, width], U32, name="w%d" % first_feature, align_bytes=64)
+            if first_feature == 0:
+                for some in both_rounds:
+                    nc.sync.dma_start(out=w[:, some, :CHUNK].bitcast(I32), in_=words[:, some, :CHUNK])
+                nc.sync.dma_start(out=w[:, :, CHUNK:].bitcast(I32), in_=words[:, :, CHUNK:])
+            else:
+                nc.sync.dma_start(out=w[:].bitcast(I32), in_=words)
             w_words.append(w)
+            first_features.append(first_feature)
+            first_feature += width
 
         position_int = keep.tile([P, TOKEN_TILES], I32)
         nc.gpsimd.iota(position_int[:], pattern=[[P, TOKEN_TILES]], base=0, channel_multiplier=1)
@@ -175,57 +178,66 @@ def tile_diffucoderattention_pa_kernel(
                 quantise(t - 1)
         quantise(TOKEN_TILES - 1)
 
-        for c in range(len(chunks)):
-            out_rows = chunks[c][1]
-            rotated = chunks[c][2]
-            accs = []
+        for group in range(len(groups)):
+            out_rows = groups[group][2]
+            rotated = groups[group][3]
+            width = out_rows.shape[1]
+            ys = []
             for t in range(TOKEN_TILES):
-                acc = psum.tile([P, CHUNK], F32, tag="bank")
-                accs.append(acc)
-            for some in pass_rounds(c):
+                y = keep.tile([P, width], F32, name="y%d_%d" % (group, t))
+                ys.append(y)
+            for c in range(width // CHUNK):
+                cols = slice(c * CHUNK, (c + 1) * CHUNK)
+                scale_cols = slice(first_features[group] + c * CHUNK, first_features[group] + (c + 1) * CHUNK)
+                accs = []
                 for t in range(TOKEN_TILES):
-                    for g in range(PASSES)[some]:
-                        nc.tensor.matmul_mx(
-                            out=accs[t][:],
-                            lhsT=x_codes[:, t, g * P : (g + 1) * P].bitcast(FP8X4),
-                            lhsT_scale=x_scales[:, t, g * P : (g + 1) * P],
-                            rhs=w_words[c][:, g, :].bitcast(FP8X4),
-                            rhs_scale=w_scales[4 * g : P, c * CHUNK : (c + 1) * CHUNK],
-                            start=(g == 0),
-                            stop=(g == PASSES - 1),
+                    acc = psum.tile([P, CHUNK], F32, tag="bank")
+                    accs.append(acc)
+                for some in both_rounds if (group == 0 and c == 0) else one_round:
+                    for t in range(TOKEN_TILES):
+                        for g in range(PASSES)[some]:
+                            nc.tensor.matmul_mx(
+                                out=accs[t][:],
+                                lhsT=x_codes[:, t, g * P : (g + 1) * P].bitcast(FP8X4),
+                                lhsT_scale=x_scales[:, t, g * P : (g + 1) * P],
+                                rhs=w_words[group][:, g, cols].bitcast(FP8X4),
+                                rhs_scale=w_scales[4 * g : P, scale_cols],
+                                start=(g == 0),
+                                stop=(g == PASSES - 1),
+                            )
+                for t in range(TOKEN_TILES):
+                    acc = accs[t]
+                    y = ys[t][:, cols]
+                    if rotated:
+                        acc_heads = acc[:].rearrange("p (h d) -> p h d", d=HEAD)
+                        y_heads = y.rearrange("p (h d) -> p h d", d=HEAD)
+                        nc.scalar.copy(out=y_heads[:, :, ROTATED:], in_=acc_heads[:, :, ROTATED:])
+                        acc_pairs = acc_heads[:, :, :ROTATED].rearrange("p h (i e) -> p h i e", e=2)
+                        y_pairs = y_heads[:, :, :ROTATED].rearrange("p h (i e) -> p h i e", e=2)
+                        plane_shape = [P, HEADS_IN_CHUNK, PAIRS]
+                        nc.vector.tensor_tensor(
+                            out=y_pairs,
+                            in0=acc_pairs,
+                            in1=trig[:, COS, t, :].unsqueeze(1).unsqueeze(3).to_broadcast(plane_shape + [2]),
+                            op=ALU.mult,
                         )
-            for t in range(TOKEN_TILES):
-                acc = accs[t]
-                y = y_pool.tile([P, CHUNK], F32, tag="y")
-                if rotated:
-                    acc_heads = acc[:].rearrange("p (h d) -> p h d", d=HEAD)
-                    y_heads = y[:].rearrange("p (h d) -> p h d", d=HEAD)
-                    nc.scalar.copy(out=y_heads[:, :, ROTATED:], in_=acc_heads[:, :, ROTATED:])
-                    acc_pairs = acc_heads[:, :, :ROTATED].rearrange("p h (i e) -> p h i e", e=2)
-                    y_pairs = y_heads[:, :, :ROTATED].rearrange("p h (i e) -> p h i e", e=2)
-                    plane_shape = [P, HEADS_IN_CHUNK, PAIRS]
-                    nc.vector.tensor_tensor(
-                        out=y_pairs,
-                        in0=acc_pairs,
-                        in1=trig[:, COS, t, :].unsqueeze(1).unsqueeze(3).to_broadcast(plane_shape + [2]),
-                        op=ALU.mult,
-                    )
-                    cross = cross_pool.tile([P, 2, HEADS_IN_CHUNK, PAIRS], F32)
-                    nc.vector.tensor_tensor(
-                        out=cross[:, 0],
-                        in0=acc_pairs[:, :, :, 1],
-                        in1=trig[:, NEG_SIN, t, :].unsqueeze(1).to_broadcast(plane_shape),
-                        op=ALU.mult,
-                    )
-                    nc.vector.tensor_tensor(
-                        out=cross[:, 1],
-                        in0=acc_pairs[:, :, :, 0],
-                        in1=trig[:, SIN, t, :].unsqueeze(1).to_broadcast(plane_shape),
-                        op=ALU.mult,
-                    )
-                    nc.vector.tensor_tensor(
-                        out=y_pairs, in0=y_pairs, in1=cross[:].rearrange("p e h i -> p h i e"), op=ALU.add
-                    )
-                else:
-                    nc.scalar.copy(out=y[:], in_=acc[:])
-                nc.sync.dma_start(out=out_rows[t * P : (t + 1) * P, :], in_=y[:])
+                        cross = cross_pool.tile([P, 2, HEADS_IN_CHUNK, PAIRS], F32)
+                        nc.vector.tensor_tensor(
+                            out=cross[:, 0],
+                            in0=acc_pairs[:, :, :, 1],
+                            in1=trig[:, NEG_SIN, t, :].unsqueeze(1).to_broadcast(plane_shape),
+                            op=ALU.mult,
+                        )
+                        nc.vector.tensor_tensor(
+                            out=cross[:, 1],
+                            in0=acc_pairs[:, :, :, 0],
+                            in1=trig[:, SIN, t, :].unsqueeze(1).to_broadcast(plane_shape),
+                            op=ALU.mult,
+                        )
+                        nc.gpsimd.tensor_tensor(
+                            out=y_pairs, in0=y_pairs, in1=cross[:].rearrange("p e h i -> p h i e"), op=ALU.add
+                        )
+                    else:
+                        nc.scalar.copy(out=y, in_=acc[:])
+                    if (c + 1) * CHUNK == width:
+                        nc.sync.dma_start(out=out_rows[t * P : (t + 1) * P, :], in_=ys[t][:])

@@ -60,13 +60,11 @@ def tile_diffucoderattention_pa_kernel(
     q_low = slice(0, Q_FEATURES // 2)
     q_high = slice(Q_FEATURES // 2, Q_FEATURES)
     groups = (
-        (words_by_partition(Wq_words)[:, :, q_low], Wq_scales, rows_by_token(out_0)[:, q_low], True),
-        (words_by_partition(Wq_words)[:, :, q_high], None, rows_by_token(out_0)[:, q_high], True),
+        (words_by_partition(Wq_words)[:, :, q_low], Wq_scales[:, :, q_low], rows_by_token(out_0)[:, q_low], True),
+        (words_by_partition(Wq_words)[:, :, q_high], Wq_scales[:, :, q_high], rows_by_token(out_0)[:, q_high], True),
         (words_by_partition(Wk_words), Wk_scales, rows_by_token(out_1), True),
         (words_by_partition(Wv_words), Wv_scales, rows_by_token(out_2), False),
     )
-    both_rounds = (slice(0, HALF_PASSES), slice(HALF_PASSES, PASSES))
-    one_round = (slice(0, PASSES),)
 
     with ExitStack() as ctx:
         keep = ctx.enter_context(tc.tile_pool(name="keep", bufs=1))
@@ -84,23 +82,23 @@ def tile_diffucoderattention_pa_kernel(
         w_words = []
         first_features = []
         first_feature = 0
-        for words, scales, out_rows, rotated in groups:
+        for group in range(len(groups)):
+            words = groups[group][0]
+            scales = groups[group][1]
             width = words.shape[2]
-            if scales is not None:
-                for quad in range(4):
-                    nc.sync.dma_start(
-                        out=w_scales[
-                            32 * quad : 32 * quad + 16, first_feature : first_feature + scales.shape[2]
-                        ].bitcast(I32),
-                        in_=scales[:, 4 * quad : 4 * quad + 4, :].bitcast(I32),
-                    )
-            w = keep.tile([P, PASSES, width], U32, name="w%d" % first_feature, align_bytes=64)
-            if first_feature == 0:
-                for some in both_rounds:
-                    nc.sync.dma_start(out=w[:, some, :CHUNK].bitcast(I32), in_=words[:, some, :CHUNK])
-                nc.sync.dma_start(out=w[:, :, CHUNK:].bitcast(I32), in_=words[:, :, CHUNK:])
-            else:
-                nc.sync.dma_start(out=w[:].bitcast(I32), in_=words)
+            for quad in range(4):
+                nc.sync.dma_start(
+                    out=w_scales[32 * quad : 32 * quad + 16, first_feature : first_feature + width].bitcast(I32),
+                    in_=scales[:, 4 * quad : 4 * quad + 4, :].bitcast(I32),
+                )
+            w = keep.tile([P, PASSES, width], U32, name="w%d" % group, align_bytes=64)
+            for c in range(width // CHUNK):
+                cols = slice(c * CHUNK, (c + 1) * CHUNK)
+                if group == 0 and c == 0:
+                    for some in (slice(0, HALF_PASSES), slice(HALF_PASSES, PASSES)):
+                        nc.sync.dma_start(out=w[:, some, cols].bitcast(I32), in_=words[:, some, cols])
+                else:
+                    nc.sync.dma_start(out=w[:, :, cols].bitcast(I32), in_=words[:, :, cols])
             w_words.append(w)
             first_features.append(first_feature)
             first_feature += width
@@ -146,15 +144,17 @@ def tile_diffucoderattention_pa_kernel(
             nc.vector.scalar_tensor_tensor(
                 out=phase[:], in0=turns[:], scalar=-part, in1=phase[:], op0=ALU.mult, op1=ALU.add
             )
-        trig = keep.tile([P, 3, TOKEN_TILES, PAIRS], F32)
-        nc.scalar.activation(out=trig[:], in_=phase[:], func=ACT.Sin)
 
         grouped = keep.tile([P, TOKEN_TILES, PASSES * P * 4], BF16, align_bytes=64)
         x_codes = keep.tile([P, TOKEN_TILES, PASSES * P], U32, align_bytes=64)
         x_scales = keep.tile([P, TOKEN_TILES, PASSES * P], U8, align_bytes=64)
 
-        def quantise(t):
-            nc.vector.quantize_mx(out=x_codes[:, t, :].bitcast(FP8X4), scales=x_scales[:, t, :], in_=grouped[:, t, :])
+        def quantise(t, half):
+            nc.vector.quantize_mx(
+                out=x_codes[:, t, 2 * P * half : 2 * P * (half + 1)].bitcast(FP8X4),
+                scales=x_scales[:, t, 2 * P * half : 2 * P * (half + 1)],
+                in_=grouped[:, t, 8 * P * half : 8 * P * (half + 1)],
+            )
 
         for t in range(TOKEN_TILES):
             x_as_words = x_sb[:, t, :].bitcast(F32)
@@ -167,16 +167,14 @@ def tile_diffucoderattention_pa_kernel(
                         nc.tensor.transpose(
                             flipped[:, g2, u, :], x_as_words[:, 256 * g + u : 256 * (g + 1) : 2], identity[:]
                         )
-                side_by_side = grouped_as_words[:, 512 * half : 512 * (half + 1)].rearrange(
+                side_by_side = grouped_as_words[:, 4 * P * half : 4 * P * (half + 1)].rearrange(
                     "p (g r u) -> p g r u", g=2, u=2
                 )
-                if half == 0:
-                    nc.vector.tensor_copy(out=side_by_side, in_=flipped[:].rearrange("p g u r -> p g r u"))
-                else:
-                    nc.scalar.copy(out=side_by_side, in_=flipped[:].rearrange("p g u r -> p g r u"))
-            if t > 0:
-                quantise(t - 1)
-        quantise(TOKEN_TILES - 1)
+                nc.scalar.copy(out=side_by_side, in_=flipped[:].rearrange("p g u r -> p g r u"))
+                quantise(t, half)
+
+        trig = keep.tile([P, 3, TOKEN_TILES, PAIRS], F32)
+        nc.scalar.activation(out=trig[:], in_=phase[:], func=ACT.Sin)
 
         for group in range(len(groups)):
             out_rows = groups[group][2]
@@ -193,18 +191,22 @@ def tile_diffucoderattention_pa_kernel(
                 for t in range(TOKEN_TILES):
                     acc = psum.tile([P, CHUNK], F32, tag="bank")
                     accs.append(acc)
-                for some in both_rounds if (group == 0 and c == 0) else one_round:
+                rounds = 2 if (group == 0 and c == 0) else 1
+                order = []
+                for first_pass in range(0, PASSES, PASSES // rounds):
                     for t in range(TOKEN_TILES):
-                        for g in range(PASSES)[some]:
-                            nc.tensor.matmul_mx(
-                                out=accs[t][:],
-                                lhsT=x_codes[:, t, g * P : (g + 1) * P].bitcast(FP8X4),
-                                lhsT_scale=x_scales[:, t, g * P : (g + 1) * P],
-                                rhs=w_words[group][:, g, cols].bitcast(FP8X4),
-                                rhs_scale=w_scales[4 * g : P, scale_cols],
-                                start=(g == 0),
-                                stop=(g == PASSES - 1),
-                            )
+                        for g in range(first_pass, first_pass + PASSES // rounds):
+                            order.append((t, g))
+                for t, g in order:
+                    nc.tensor.matmul_mx(
+                        out=accs[t][:],
+                        lhsT=x_codes[:, t, g * P : (g + 1) * P].bitcast(FP8X4),
+                        lhsT_scale=x_scales[:, t, g * P : (g + 1) * P],
+                        rhs=w_words[group][:, g, cols].bitcast(FP8X4),
+                        rhs_scale=w_scales[4 * g : P, scale_cols],
+                        start=(g == 0),
+                        stop=(g == PASSES - 1),
+                    )
                 for t in range(TOKEN_TILES):
                     acc = accs[t]
                     y = ys[t][:, cols]

@@ -42,6 +42,9 @@ NEG_SIN = 0
 SIN = 1
 COS = 2
 
+WARM_FIRST = 6
+WARM_BETWEEN = 2
+
 FLOPS = 2 * TOKENS * K * FEATURES
 
 
@@ -71,6 +74,14 @@ def tile_diffucoderattention_pa_kernel(
         cross_pool = ctx.enter_context(tc.tile_pool(name="cross", bufs=3))
         psum = ctx.enter_context(tc.psum_pool(name="psum", bufs=8))
         ctx.enter_context(tc.manual_schedule())
+
+        warm = keep.tile([P, CHUNK], BF16)
+        nc.vector.memset(warm[:], 0.0)
+        warm_bank = psum.tile([P, CHUNK], F32, tag="bank")
+
+        def keep_warm(count):
+            for i in range(count):
+                nc.tensor.matmul(out=warm_bank[:], lhsT=warm[:, 0:P], rhs=warm[:], start=True, stop=True)
 
         x_sb = keep.tile([P, TOKEN_TILES, K], BF16)
         for t in range(TOKEN_TILES):
@@ -156,7 +167,10 @@ def tile_diffucoderattention_pa_kernel(
                 in_=grouped[:, t, 8 * P * half : 8 * P * (half + 1)],
             )
 
+        keep_warm(WARM_FIRST)
         for t in range(TOKEN_TILES):
+            if t > 0:
+                keep_warm(WARM_BETWEEN)
             x_as_words = x_sb[:, t, :].bitcast(F32)
             grouped_as_words = grouped[:, t, :].bitcast(F32)
             for half in range(2):

@@ -43,7 +43,6 @@ SIN = 1
 COS = 2
 
 WARM_FIRST = 6
-WARM_BETWEEN = 2
 
 FLOPS = 2 * TOKENS * K * FEATURES
 
@@ -68,6 +67,7 @@ def tile_diffucoderattention_pa_kernel(
         (words_by_partition(Wk_words), Wk_scales, rows_by_token(out_1), True),
         (words_by_partition(Wv_words), Wv_scales, rows_by_token(out_2), False),
     )
+    LAST_TILE = TOKEN_TILES - 1
 
     with ExitStack() as ctx:
         keep = ctx.enter_context(tc.tile_pool(name="keep", bufs=1))
@@ -78,13 +78,12 @@ def tile_diffucoderattention_pa_kernel(
         warm = keep.tile([P, CHUNK], BF16)
         nc.vector.memset(warm[:], 0.0)
         warm_bank = psum.tile([P, CHUNK], F32, tag="bank")
-
-        def keep_warm(count):
-            for i in range(count):
-                nc.tensor.matmul(out=warm_bank[:], lhsT=warm[:, 0:P], rhs=warm[:], start=True, stop=True)
+        for i in range(WARM_FIRST):
+            nc.tensor.matmul(out=warm_bank[:], lhsT=warm[:, 0:P], rhs=warm[:], start=True, stop=True)
 
         x_sb = keep.tile([P, TOKEN_TILES, K], BF16)
-        for t in range(TOKEN_TILES):
+
+        def load_x(t):
             nc.sync.dma_start(out=x_sb[:, t, :], in_=x[t * P : (t + 1) * P, :])
 
         w_scales = keep.tile([P, FEATURES], U8, align_bytes=64)
@@ -94,25 +93,37 @@ def tile_diffucoderattention_pa_kernel(
         first_features = []
         first_feature = 0
         for group in range(len(groups)):
-            words = groups[group][0]
-            scales = groups[group][1]
-            width = words.shape[2]
-            for quad in range(4):
-                nc.sync.dma_start(
-                    out=w_scales[32 * quad : 32 * quad + 16, first_feature : first_feature + width].bitcast(I32),
-                    in_=scales[:, 4 * quad : 4 * quad + 4, :].bitcast(I32),
-                )
+            width = groups[group][0].shape[2]
             w = keep.tile([P, PASSES, width], U32, name="w%d" % group, align_bytes=64)
-            for c in range(width // CHUNK):
-                cols = slice(c * CHUNK, (c + 1) * CHUNK)
-                if group == 0 and c == 0:
-                    for some in (slice(0, HALF_PASSES), slice(HALF_PASSES, PASSES)):
-                        nc.sync.dma_start(out=w[:, some, cols].bitcast(I32), in_=words[:, some, cols])
-                else:
-                    nc.sync.dma_start(out=w[:, :, cols].bitcast(I32), in_=words[:, :, cols])
             w_words.append(w)
             first_features.append(first_feature)
             first_feature += width
+
+        def load_scales(group):
+            scales = groups[group][1]
+            first = first_features[group]
+            width = scales.shape[2]
+            for quad in range(4):
+                nc.sync.dma_start(
+                    out=w_scales[32 * quad : 32 * quad + 16, first : first + width].bitcast(I32),
+                    in_=scales[:, 4 * quad : 4 * quad + 4, :].bitcast(I32),
+                )
+
+        def load_words(group, c, some):
+            cols = slice(c * CHUNK, (c + 1) * CHUNK)
+            nc.sync.dma_start(out=w_words[group][:, some, cols].bitcast(I32), in_=groups[group][0][:, some, cols])
+
+        for t in range(LAST_TILE):
+            load_x(t)
+        load_scales(0)
+        load_words(0, 0, slice(0, HALF_PASSES))
+        load_x(LAST_TILE)
+        load_words(0, 0, slice(HALF_PASSES, PASSES))
+        load_words(0, 1, slice(0, PASSES))
+        for group in range(1, len(groups)):
+            load_scales(group)
+            for c in range(groups[group][0].shape[2] // CHUNK):
+                load_words(group, c, slice(0, PASSES))
 
         position_int = keep.tile([P, TOKEN_TILES], I32)
         nc.gpsimd.iota(position_int[:], pattern=[[P, TOKEN_TILES]], base=0, channel_multiplier=1)
@@ -155,22 +166,13 @@ def tile_diffucoderattention_pa_kernel(
             nc.vector.scalar_tensor_tensor(
                 out=phase[:], in0=turns[:], scalar=-part, in1=phase[:], op0=ALU.mult, op1=ALU.add
             )
+        trig = keep.tile([P, 3, TOKEN_TILES, PAIRS], F32)
 
         grouped = keep.tile([P, TOKEN_TILES, PASSES * P * 4], BF16, align_bytes=64)
         x_codes = keep.tile([P, TOKEN_TILES, PASSES * P], U32, align_bytes=64)
         x_scales = keep.tile([P, TOKEN_TILES, PASSES * P], U8, align_bytes=64)
 
-        def quantise(t, half):
-            nc.vector.quantize_mx(
-                out=x_codes[:, t, 2 * P * half : 2 * P * (half + 1)].bitcast(FP8X4),
-                scales=x_scales[:, t, 2 * P * half : 2 * P * (half + 1)],
-                in_=grouped[:, t, 8 * P * half : 8 * P * (half + 1)],
-            )
-
-        keep_warm(WARM_FIRST)
-        for t in range(TOKEN_TILES):
-            if t > 0:
-                keep_warm(WARM_BETWEEN)
+        def flip_and_quantise(t):
             x_as_words = x_sb[:, t, :].bitcast(F32)
             grouped_as_words = grouped[:, t, :].bitcast(F32)
             for half in range(2):
@@ -185,10 +187,60 @@ def tile_diffucoderattention_pa_kernel(
                     "p (g r u) -> p g r u", g=2, u=2
                 )
                 nc.scalar.copy(out=side_by_side, in_=flipped[:].rearrange("p g u r -> p g r u"))
-                quantise(t, half)
+                nc.vector.quantize_mx(
+                    out=x_codes[:, t, 2 * P * half : 2 * P * (half + 1)].bitcast(FP8X4),
+                    scales=x_scales[:, t, 2 * P * half : 2 * P * (half + 1)],
+                    in_=grouped[:, t, 8 * P * half : 8 * P * (half + 1)],
+                )
 
-        trig = keep.tile([P, 3, TOKEN_TILES, PAIRS], F32)
-        nc.scalar.activation(out=trig[:], in_=phase[:], func=ACT.Sin)
+        def passes(acc, t, some, group, c):
+            first = first_features[group] + c * CHUNK
+            for g in some:
+                nc.tensor.matmul_mx(
+                    out=acc[:],
+                    lhsT=x_codes[:, t, g * P : (g + 1) * P].bitcast(FP8X4),
+                    lhsT_scale=x_scales[:, t, g * P : (g + 1) * P],
+                    rhs=w_words[group][:, g, c * CHUNK : (c + 1) * CHUNK].bitcast(FP8X4),
+                    rhs_scale=w_scales[4 * g : P, first : first + CHUNK],
+                    start=(g == 0),
+                    stop=(g == PASSES - 1),
+                )
+
+        def empty_bank(acc, y, t, rotated):
+            if not rotated:
+                nc.scalar.copy(out=y, in_=acc[:])
+                return
+            acc_heads = acc[:].rearrange("p (h d) -> p h d", d=HEAD)
+            y_heads = y.rearrange("p (h d) -> p h d", d=HEAD)
+            nc.scalar.copy(out=y_heads[:, :, ROTATED:], in_=acc_heads[:, :, ROTATED:])
+            acc_pairs = acc_heads[:, :, :ROTATED].rearrange("p h (i e) -> p h i e", e=2)
+            y_pairs = y_heads[:, :, :ROTATED].rearrange("p h (i e) -> p h i e", e=2)
+            plane_shape = [P, HEADS_IN_CHUNK, PAIRS]
+            nc.vector.tensor_tensor(
+                out=y_pairs,
+                in0=acc_pairs,
+                in1=trig[:, COS, t, :].unsqueeze(1).unsqueeze(3).to_broadcast(plane_shape + [2]),
+                op=ALU.mult,
+            )
+            cross = cross_pool.tile([P, 2, HEADS_IN_CHUNK, PAIRS], F32)
+            nc.vector.tensor_tensor(
+                out=cross[:, 0],
+                in0=acc_pairs[:, :, :, 1],
+                in1=trig[:, NEG_SIN, t, :].unsqueeze(1).to_broadcast(plane_shape),
+                op=ALU.mult,
+            )
+            nc.vector.tensor_tensor(
+                out=cross[:, 1],
+                in0=acc_pairs[:, :, :, 0],
+                in1=trig[:, SIN, t, :].unsqueeze(1).to_broadcast(plane_shape),
+                op=ALU.mult,
+            )
+            nc.gpsimd.tensor_tensor(
+                out=y_pairs, in0=y_pairs, in1=cross[:].rearrange("p e h i -> p h i e"), op=ALU.add
+            )
+
+        for t in range(LAST_TILE):
+            flip_and_quantise(t)
 
         for group in range(len(groups)):
             out_rows = groups[group][2]
@@ -199,61 +251,25 @@ def tile_diffucoderattention_pa_kernel(
                 y = keep.tile([P, width], F32, name="y%d_%d" % (group, t))
                 ys.append(y)
             for c in range(width // CHUNK):
-                cols = slice(c * CHUNK, (c + 1) * CHUNK)
-                scale_cols = slice(first_features[group] + c * CHUNK, first_features[group] + (c + 1) * CHUNK)
                 accs = []
-                for t in range(TOKEN_TILES):
+                if group == 0 and c == 0:
+                    for t in range(LAST_TILE):
+                        acc = psum.tile([P, CHUNK], F32, tag="bank")
+                        accs.append(acc)
+                        passes(acc, t, range(0, HALF_PASSES), group, c)
+                    flip_and_quantise(LAST_TILE)
+                    nc.scalar.activation(out=trig[:], in_=phase[:], func=ACT.Sin)
+                    for t in range(LAST_TILE):
+                        passes(accs[t], t, range(HALF_PASSES, PASSES), group, c)
                     acc = psum.tile([P, CHUNK], F32, tag="bank")
                     accs.append(acc)
-                rounds = 2 if (group == 0 and c == 0) else 1
-                order = []
-                for first_pass in range(0, PASSES, PASSES // rounds):
+                    passes(acc, LAST_TILE, range(PASSES), group, c)
+                else:
                     for t in range(TOKEN_TILES):
-                        for g in range(first_pass, first_pass + PASSES // rounds):
-                            order.append((t, g))
-                for t, g in order:
-                    nc.tensor.matmul_mx(
-                        out=accs[t][:],
-                        lhsT=x_codes[:, t, g * P : (g + 1) * P].bitcast(FP8X4),
-                        lhsT_scale=x_scales[:, t, g * P : (g + 1) * P],
-                        rhs=w_words[group][:, g, cols].bitcast(FP8X4),
-                        rhs_scale=w_scales[4 * g : P, scale_cols],
-                        start=(g == 0),
-                        stop=(g == PASSES - 1),
-                    )
+                        acc = psum.tile([P, CHUNK], F32, tag="bank")
+                        accs.append(acc)
+                        passes(acc, t, range(PASSES), group, c)
                 for t in range(TOKEN_TILES):
-                    acc = accs[t]
-                    y = ys[t][:, cols]
-                    if rotated:
-                        acc_heads = acc[:].rearrange("p (h d) -> p h d", d=HEAD)
-                        y_heads = y.rearrange("p (h d) -> p h d", d=HEAD)
-                        nc.scalar.copy(out=y_heads[:, :, ROTATED:], in_=acc_heads[:, :, ROTATED:])
-                        acc_pairs = acc_heads[:, :, :ROTATED].rearrange("p h (i e) -> p h i e", e=2)
-                        y_pairs = y_heads[:, :, :ROTATED].rearrange("p h (i e) -> p h i e", e=2)
-                        plane_shape = [P, HEADS_IN_CHUNK, PAIRS]
-                        nc.vector.tensor_tensor(
-                            out=y_pairs,
-                            in0=acc_pairs,
-                            in1=trig[:, COS, t, :].unsqueeze(1).unsqueeze(3).to_broadcast(plane_shape + [2]),
-                            op=ALU.mult,
-                        )
-                        cross = cross_pool.tile([P, 2, HEADS_IN_CHUNK, PAIRS], F32)
-                        nc.vector.tensor_tensor(
-                            out=cross[:, 0],
-                            in0=acc_pairs[:, :, :, 1],
-                            in1=trig[:, NEG_SIN, t, :].unsqueeze(1).to_broadcast(plane_shape),
-                            op=ALU.mult,
-                        )
-                        nc.vector.tensor_tensor(
-                            out=cross[:, 1],
-                            in0=acc_pairs[:, :, :, 0],
-                            in1=trig[:, SIN, t, :].unsqueeze(1).to_broadcast(plane_shape),
-                            op=ALU.mult,
-                        )
-                        nc.gpsimd.tensor_tensor(
-                            out=y_pairs, in0=y_pairs, in1=cross[:].rearrange("p e h i -> p h i e"), op=ALU.add
-                        )
-                    else:
-                        nc.scalar.copy(out=y, in_=acc[:])
+                    empty_bank(accs[t], ys[t][:, c * CHUNK : (c + 1) * CHUNK], t, rotated)
                     if (c + 1) * CHUNK == width:
                         nc.sync.dma_start(out=out_rows[t * P : (t + 1) * P, :], in_=ys[t][:])

@@ -43,6 +43,7 @@ SIN = 1
 COS = 2
 
 WARM_FIRST = 6
+WARM_BETWEEN = 2
 
 FLOPS = 2 * TOKENS * K * FEATURES
 
@@ -68,6 +69,7 @@ def tile_diffucoderattention_pa_kernel(
         (words_by_partition(Wv_words), Wv_scales, rows_by_token(out_2), False),
     )
     LAST_TILE = TOKEN_TILES - 1
+    LAST_PIECES = (slice(0, 256), slice(256, 512))
 
     with ExitStack() as ctx:
         keep = ctx.enter_context(tc.tile_pool(name="keep", bufs=1))
@@ -78,8 +80,12 @@ def tile_diffucoderattention_pa_kernel(
         warm = keep.tile([P, CHUNK], BF16)
         nc.vector.memset(warm[:], 0.0)
         warm_bank = psum.tile([P, CHUNK], F32, tag="bank")
-        for i in range(WARM_FIRST):
-            nc.tensor.matmul(out=warm_bank[:], lhsT=warm[:, 0:P], rhs=warm[:], start=True, stop=True)
+
+        def keep_warm(count):
+            for i in range(count):
+                nc.tensor.matmul(out=warm_bank[:], lhsT=warm[:, 0:P], rhs=warm[:], start=True, stop=True)
+
+        keep_warm(WARM_FIRST)
 
         x_sb = keep.tile([P, TOKEN_TILES, K], BF16)
 
@@ -193,15 +199,17 @@ def tile_diffucoderattention_pa_kernel(
                     in_=grouped[:, t, 8 * P * half : 8 * P * (half + 1)],
                 )
 
-        def passes(acc, t, some, group, c):
-            first = first_features[group] + c * CHUNK
+        def passes(acc, t, some, group, c, piece=slice(0, CHUNK)):
+            low = c * CHUNK + piece.start
+            high = c * CHUNK + piece.stop
+            first = first_features[group]
             for g in some:
                 nc.tensor.matmul_mx(
                     out=acc[:],
                     lhsT=x_codes[:, t, g * P : (g + 1) * P].bitcast(FP8X4),
                     lhsT_scale=x_scales[:, t, g * P : (g + 1) * P],
-                    rhs=w_words[group][:, g, c * CHUNK : (c + 1) * CHUNK].bitcast(FP8X4),
-                    rhs_scale=w_scales[4 * g : P, first : first + CHUNK],
+                    rhs=w_words[group][:, g, low:high].bitcast(FP8X4),
+                    rhs_scale=w_scales[4 * g : P, first + low : first + high],
                     start=(g == 0),
                     stop=(g == PASSES - 1),
                 )
@@ -241,6 +249,7 @@ def tile_diffucoderattention_pa_kernel(
 
         for t in range(LAST_TILE):
             flip_and_quantise(t)
+            keep_warm(WARM_BETWEEN)
 
         for group in range(len(groups)):
             out_rows = groups[group][2]
@@ -264,6 +273,23 @@ def tile_diffucoderattention_pa_kernel(
                     acc = psum.tile([P, CHUNK], F32, tag="bank")
                     accs.append(acc)
                     passes(acc, LAST_TILE, range(PASSES), group, c)
+                elif group == len(groups) - 1:
+                    for t in range(LAST_TILE):
+                        acc = psum.tile([P, CHUNK], F32, tag="bank")
+                        accs.append(acc)
+                        passes(acc, t, range(PASSES), group, c)
+                    for piece in LAST_PIECES:
+                        acc = psum.tile([P, piece.stop - piece.start], F32, tag="bank")
+                        accs.append(acc)
+                        passes(acc, LAST_TILE, range(PASSES), group, c, piece)
+                    for t in range(LAST_TILE):
+                        empty_bank(accs[t], ys[t][:], t, rotated)
+                        nc.sync.dma_start(out=out_rows[t * P : (t + 1) * P, :], in_=ys[t][:])
+                    for i in range(len(LAST_PIECES)):
+                        piece = LAST_PIECES[i]
+                        empty_bank(accs[LAST_TILE + i], ys[LAST_TILE][:, piece], LAST_TILE, rotated)
+                        nc.sync.dma_start(out=out_rows[LAST_TILE * P :, piece], in_=ys[LAST_TILE][:, piece])
+                    continue
                 else:
                     for t in range(TOKEN_TILES):
                         acc = psum.tile([P, CHUNK], F32, tag="bank")

@@ -42,7 +42,7 @@ NEG_SIN = 0
 SIN = 1
 COS = 2
 
-WARM_FIRST = 6
+WARM_FIRST = 4
 WARM_BETWEEN = 2
 
 FLOPS = 2 * TOKENS * K * FEATURES
@@ -70,6 +70,7 @@ def tile_diffucoderattention_pa_kernel(
     )
     LAST_TILE = TOKEN_TILES - 1
     LAST_PIECES = (slice(0, 256), slice(256, 512))
+    X_PIECES = (4, 2, 1, 1)
 
     with ExitStack() as ctx:
         keep = ctx.enter_context(tc.tile_pool(name="keep", bufs=1))
@@ -90,7 +91,9 @@ def tile_diffucoderattention_pa_kernel(
         x_sb = keep.tile([P, TOKEN_TILES, K], BF16)
 
         def load_x(t):
-            nc.sync.dma_start(out=x_sb[:, t, :], in_=x[t * P : (t + 1) * P, :])
+            step = K // X_PIECES[t]
+            for first in range(0, K, step):
+                nc.sync.dma_start(out=x_sb[:, t, first : first + step], in_=x[t * P : (t + 1) * P, first : first + step])
 
         w_scales = keep.tile([P, FEATURES], U8, align_bytes=64)
         nc.vector.memset(w_scales[:].bitcast(I32), 0)

@@ -18,7 +18,6 @@ TOKENS = 512
 K = 2048
 K_PASS = 512
 PASSES = K // K_PASS
-HALF_PASSES = PASSES // 2
 TOKEN_TILES = TOKENS // P
 CHUNK = 512
 HEAD = 128
@@ -122,12 +121,11 @@ def tile_diffucoderattention_pa_kernel(
             cols = slice(c * CHUNK, (c + 1) * CHUNK)
             nc.sync.dma_start(out=w_words[group][:, some, cols].bitcast(I32), in_=groups[group][0][:, some, cols])
 
-        for t in range(LAST_TILE):
+        for t in range(TOKEN_TILES):
             load_x(t)
         load_scales(0)
-        load_words(0, 0, slice(0, HALF_PASSES))
-        load_x(LAST_TILE)
-        load_words(0, 0, slice(HALF_PASSES, PASSES))
+        for g in range(PASSES):
+            load_words(0, 0, slice(g, g + 1))
         load_words(0, 1, slice(0, PASSES))
         for group in range(1, len(groups)):
             load_scales(group)
@@ -250,9 +248,11 @@ def tile_diffucoderattention_pa_kernel(
                 out=y_pairs, in0=y_pairs, in1=cross[:].rearrange("p e h i -> p h i e"), op=ALU.add
             )
 
-        for t in range(LAST_TILE):
+        for t in range(TOKEN_TILES):
             flip_and_quantise(t)
-            keep_warm(WARM_BETWEEN)
+            if t != LAST_TILE:
+                keep_warm(WARM_BETWEEN)
+        nc.scalar.activation(out=trig[:], in_=phase[:], func=ACT.Sin)
 
         for group in range(len(groups)):
             out_rows = groups[group][2]
@@ -265,17 +265,12 @@ def tile_diffucoderattention_pa_kernel(
             for c in range(width // CHUNK):
                 accs = []
                 if group == 0 and c == 0:
-                    for t in range(LAST_TILE):
+                    for t in range(TOKEN_TILES):
                         acc = psum.tile([P, CHUNK], F32, tag="bank")
                         accs.append(acc)
-                        passes(acc, t, range(0, HALF_PASSES), group, c)
-                    flip_and_quantise(LAST_TILE)
-                    nc.scalar.activation(out=trig[:], in_=phase[:], func=ACT.Sin)
-                    for t in range(LAST_TILE):
-                        passes(accs[t], t, range(HALF_PASSES, PASSES), group, c)
-                    acc = psum.tile([P, CHUNK], F32, tag="bank")
-                    accs.append(acc)
-                    passes(acc, LAST_TILE, range(PASSES), group, c)
+                    for g in range(PASSES):
+                        for t in range(TOKEN_TILES):
+                            passes(accs[t], t, range(g, g + 1), group, c)
                 elif group == len(groups) - 1:
                     for t in range(LAST_TILE):
                         acc = psum.tile([P, CHUNK], F32, tag="bank")

@@ -42,7 +42,7 @@ SIN = 1
 COS = 2
 
 WARM_FIRST = 4
-WARM_BETWEEN = 2
+WARM_BETWEEN = (2, 0, 2, 0)
 
 FLOPS = 2 * TOKENS * K * FEATURES
 
@@ -250,8 +250,7 @@ def tile_diffucoderattention_pa_kernel(
 
         for t in range(TOKEN_TILES):
             flip_and_quantise(t)
-            if t != LAST_TILE:
-                keep_warm(WARM_BETWEEN)
+            keep_warm(WARM_BETWEEN[t])
         nc.scalar.activation(out=trig[:], in_=phase[:], func=ACT.Sin)
 
         for group in range(len(groups)):

@@ -69,7 +69,7 @@ def tile_diffucoderattention_pa_kernel(
     )
     LAST_TILE = TOKEN_TILES - 1
     LAST_PIECES = (slice(0, 256), slice(256, 512))
-    X_PIECES = (4, 2, 1, 1)
+    X_PIECES = (4, 2, 2, 2)
 
     with ExitStack() as ctx:
         keep = ctx.enter_context(tc.tile_pool(name="keep", bufs=1))
@@ -94,7 +94,7 @@ def tile_diffucoderattention_pa_kernel(
             for first in range(0, K, step):
                 nc.sync.dma_start(out=x_sb[:, t, first : first + step], in_=x[t * P : (t + 1) * P, first : first + step])
 
-        w_scales = keep.tile([P, FEATURES], U8, align_bytes=64)
+        w_scales = keep.tile([P, FEATURES], U8, align_bytes=256)
         nc.vector.memset(w_scales[:].bitcast(I32), 0)
 
         w_words = []
@@ -102,7 +102,7 @@ def tile_diffucoderattention_pa_kernel(
         first_feature = 0
         for group in range(len(groups)):
             width = groups[group][0].shape[2]
-            w = keep.tile([P, PASSES, width], U32, name="w%d" % group, align_bytes=64)
+            w = keep.tile([P, PASSES, width], U32, name="w%d" % group, align_bytes=256)
             w_words.append(w)
             first_features.append(first_feature)
             first_feature += width
@@ -175,9 +175,9 @@ def tile_diffucoderattention_pa_kernel(
             )
         trig = keep.tile([P, 3, TOKEN_TILES, PAIRS], F32)
 
-        grouped = keep.tile([P, TOKEN_TILES, PASSES * P * 4], BF16, align_bytes=64)
-        x_codes = keep.tile([P, TOKEN_TILES, PASSES * P], U32, align_bytes=64)
-        x_scales = keep.tile([P, TOKEN_TILES, PASSES * P], U8, align_bytes=64)
+        grouped = keep.tile([P, TOKEN_TILES, PASSES * P * 4], BF16, align_bytes=256)
+        x_codes = keep.tile([P, TOKEN_TILES, PASSES * P], U32, align_bytes=256)
+        x_scales = keep.tile([P, TOKEN_TILES, PASSES * P], U8, align_bytes=256)
 
         def flip_and_quantise(t):
             x_as_words = x_sb[:, t, :].bitcast(F32)

@@ -124,9 +124,9 @@ def tile_diffucoderattention_pa_kernel(
         for t in range(TOKEN_TILES):
             load_x(t)
         load_scales(0)
-        for g in range(PASSES):
-            load_words(0, 0, slice(g, g + 1))
-        load_words(0, 1, slice(0, PASSES))
+        for c in range(2):
+            for g in range(PASSES):
+                load_words(0, c, slice(g, g + 1))
         for group in range(1, len(groups)):
             load_scales(group)
             for c in range(groups[group][0].shape[2] // CHUNK):
@@ -263,7 +263,7 @@ def tile_diffucoderattention_pa_kernel(
                 ys.append(y)
             for c in range(width // CHUNK):
                 accs = []
-                if group == 0 and c == 0:
+                if group == 0:
                     for t in range(TOKEN_TILES):
                         acc = psum.tile([P, CHUNK], F32, tag="bank")
                         accs.append(acc)

import math
from contextlib import ExitStack

import concourse.mybir as mybir
from concourse.masks import make_identity

F32 = mybir.dt.float32
BF16 = mybir.dt.bfloat16
I32 = mybir.dt.int32
U32 = mybir.dt.uint32
U8 = mybir.dt.uint8
FP8X4 = mybir.dt.float8_e4m3fn_x4
ALU = mybir.AluOpType
ACT = mybir.ActivationFunctionType

P = 128
TOKENS = 512
K = 2048
K_PASS = 512
PASSES = K // K_PASS
TOKEN_TILES = TOKENS // P
CHUNK = 512
HEAD = 128
HEADS_IN_CHUNK = CHUNK // HEAD
ROTATED = 64
PAIRS = ROTATED // 2
Q_FEATURES = 2048
KV_FEATURES = 512
FEATURES = Q_FEATURES + 2 * KV_FEATURES

THETA = 10000.0
FREQ_RATIO = THETA ** (-1.0 / PAIRS)

ROUND_MAGIC = 12582912.0
TWO_PI = 2.0 * math.pi
TWO_PI_HIGH = 6.28125
TWO_PI_MID = math.floor((TWO_PI - TWO_PI_HIGH) * 2.0**26) / 2.0**26
TWO_PI_LOW = TWO_PI - TWO_PI_HIGH - TWO_PI_MID

NEG_SIN = 0
SIN = 1
COS = 2

WARM_FIRST = 4
WARM_BETWEEN = (2, 0, 2, 0)

FLOPS = 2 * TOKENS * K * FEATURES


def tile_diffucoderattention_pa_kernel(
    tc, hidden_states, Wq_words, Wq_scales, Wk_words, Wk_scales, Wv_words, Wv_scales, out_0, out_1, out_2
):
    nc = tc.nc
    x = hidden_states.flatten_outer_dims()

    def words_by_partition(words):
        return words.rearrange("g p n t -> p g (n t)").bitcast(I32)

    def rows_by_token(out):
        return out.rearrange("b s h d -> (b s) (h d)")

    q_low = slice(0, Q_FEATURES // 2)
    q_high = slice(Q_FEATURES // 2, Q_FEATURES)
    groups = (
        (words_by_partition(Wq_words)[:, :, q_low], Wq_scales[:, :, q_low], rows_by_token(out_0)[:, q_low], True),
        (words_by_partition(Wq_words)[:, :, q_high], Wq_scales[:, :, q_high], rows_by_token(out_0)[:, q_high], True),
        (words_by_partition(Wk_words), Wk_scales, rows_by_token(out_1), True),
        (words_by_partition(Wv_words), Wv_scales, rows_by_token(out_2), False),
    )
    LAST_TILE = TOKEN_TILES - 1
    LAST_PIECES = (slice(0, 256), slice(256, 512))
    X_PIECES = (4, 2, 2, 2)

    with ExitStack() as ctx:
        keep = ctx.enter_context(tc.tile_pool(name="keep", bufs=1))
        cross_pool = ctx.enter_context(tc.tile_pool(name="cross", bufs=3))
        psum = ctx.enter_context(tc.psum_pool(name="psum", bufs=8))
        ctx.enter_context(tc.manual_schedule())

        warm = keep.tile([P, CHUNK], BF16)
        nc.vector.memset(warm[:], 0.0)
        warm_bank = psum.tile([P, CHUNK], F32, tag="bank")

        def keep_warm(count):
            for i in range(count):
                nc.tensor.matmul(out=warm_bank[:], lhsT=warm[:, 0:P], rhs=warm[:], start=True, stop=True)

        keep_warm(WARM_FIRST)

        x_sb = keep.tile([P, TOKEN_TILES, K], BF16)

        def load_x(t):
            step = K // X_PIECES[t]
            for first in range(0, K, step):
                nc.sync.dma_start(out=x_sb[:, t, first : first + step], in_=x[t * P : (t + 1) * P, first : first + step])

        w_scales = keep.tile([P, FEATURES], U8, align_bytes=256)
        nc.vector.memset(w_scales[:].bitcast(I32), 0)

        w_words = []
        first_features = []
        first_feature = 0
        for group in range(len(groups)):
            width = groups[group][0].shape[2]
            w = keep.tile([P, PASSES, width], U32, name="w%d" % group, align_bytes=256)
            w_words.append(w)
            first_features.append(first_feature)
            first_feature += width

        def load_scales(group):
            scales = groups[group][1]
            first = first_features[group]
            width = scales.shape[2]
            for quad in range(4):
                nc.sync.dma_start(
                    out=w_scales[32 * quad : 32 * quad + 16, first : first + width].bitcast(I32),
                    in_=scales[:, 4 * quad : 4 * quad + 4, :].bitcast(I32),
                )

        def load_words(group, c, some):
            cols = slice(c * CHUNK, (c + 1) * CHUNK)
            nc.sync.dma_start(out=w_words[group][:, some, cols].bitcast(I32), in_=groups[group][0][:, some, cols])

        for t in range(TOKEN_TILES):
            load_x(t)
        load_scales(0)
        for c in range(2):
            for g in range(PASSES):
                load_words(0, c, slice(g, g + 1))
        for group in range(1, len(groups)):
            load_scales(group)
            for c in range(groups[group][0].shape[2] // CHUNK):
                load_words(group, c, slice(0, PASSES))

        position_int = keep.tile([P, TOKEN_TILES], I32)
        nc.gpsimd.iota(position_int[:], pattern=[[P, TOKEN_TILES]], base=0, channel_multiplier=1)
        identity = keep.tile([P, P], F32)
        make_identity(nc, identity[:])

        freq = keep.tile([P, PAIRS], F32)
        nc.vector.memset(freq[:, 0:1], 1.0)
        early_sin = keep.tile([P, 1], F32)
        nc.scalar.activation(out=early_sin[:], in_=freq[:, 0:1], func=ACT.Sin)
        for doubling in range(5):
            width = 2**doubling
            nc.vector.tensor_scalar(
                out=freq[:, width : 2 * width],
                in0=freq[:, 0:width],
                scalar1=FREQ_RATIO**width,
                scalar2=None,
                op0=ALU.mult,
            )
        position = keep.tile([P, TOKEN_TILES], F32)
        nc.vector.tensor_copy(out=position[:], in_=position_int[:])
        table_shape = [P, TOKEN_TILES, PAIRS]
        phase = keep.tile([P, 3, TOKEN_TILES, PAIRS], F32)
        nc.vector.tensor_tensor(
            out=phase[:, SIN],
            in0=position[:].unsqueeze(2).to_broadcast(table_shape),
            in1=freq[:].unsqueeze(1).to_broadcast(table_shape),
            op=ALU.mult,
        )
        nc.vector.tensor_scalar(out=phase[:, NEG_SIN], in0=phase[:, SIN], scalar1=-1.0, scalar2=None, op0=ALU.mult)
        nc.vector.tensor_scalar(
            out=phase[:, COS], in0=phase[:, SIN], scalar1=math.pi / 2.0, scalar2=None, op0=ALU.add
        )
        turns = keep.tile([P, 3, TOKEN_TILES, PAIRS], F32)
        nc.vector.tensor_scalar(
            out=turns[:], in0=phase[:], scalar1=1.0 / TWO_PI, scalar2=ROUND_MAGIC, op0=ALU.mult, op1=ALU.add
        )
        nc.vector.tensor_scalar(out=turns[:], in0=turns[:], scalar1=ROUND_MAGIC, scalar2=None, op0=ALU.subtract)
        for part in (TWO_PI_HIGH, TWO_PI_MID, TWO_PI_LOW):
            nc.vector.scalar_tensor_tensor(
                out=phase[:], in0=turns[:], scalar=-part, in1=phase[:], op0=ALU.mult, op1=ALU.add
            )
        trig = keep.tile([P, 3, TOKEN_TILES, PAIRS], F32)

        grouped = keep.tile([P, TOKEN_TILES, PASSES * P * 4], BF16, align_bytes=256)
        x_codes = keep.tile([P, TOKEN_TILES, PASSES * P], U32, align_bytes=256)
        x_scales = keep.tile([P, TOKEN_TILES, PASSES * P], U8, align_bytes=256)

        def flip_and_quantise(t):
            x_as_words = x_sb[:, t, :].bitcast(F32)
            grouped_as_words = grouped[:, t, :].bitcast(F32)
            for half in range(2):
                flipped = psum.tile([P, 2, 2, P], F32, tag="bank")
                for g2 in range(2):
                    g = 2 * half + g2
                    for u in range(2):
                        nc.tensor.transpose(
                            flipped[:, g2, u, :], x_as_words[:, 256 * g + u : 256 * (g + 1) : 2], identity[:]
                        )
                side_by_side = grouped_as_words[:, 4 * P * half : 4 * P * (half + 1)].rearrange(
                    "p (g r u) -> p g r u", g=2, u=2
                )
                nc.scalar.copy(out=side_by_side, in_=flipped[:].rearrange("p g u r -> p g r u"))
                nc.vector.quantize_mx(
                    out=x_codes[:, t, 2 * P * half : 2 * P * (half + 1)].bitcast(FP8X4),
                    scales=x_scales[:, t, 2 * P * half : 2 * P * (half + 1)],
                    in_=grouped[:, t, 8 * P * half : 8 * P * (half + 1)],
                )

        def passes(acc, t, some, group, c, piece=slice(0, CHUNK)):
            low = c * CHUNK + piece.start
            high = c * CHUNK + piece.stop
            first = first_features[group]
            for g in some:
                nc.tensor.matmul_mx(
                    out=acc[:],
                    lhsT=x_codes[:, t, g * P : (g + 1) * P].bitcast(FP8X4),
                    lhsT_scale=x_scales[:, t, g * P : (g + 1) * P],
                    rhs=w_words[group][:, g, low:high].bitcast(FP8X4),
                    rhs_scale=w_scales[4 * g : P, first + low : first + high],
                    start=(g == 0),
                    stop=(g == PASSES - 1),
                )

        def empty_bank(acc, y, t, rotated):
            if not rotated:
                nc.scalar.copy(out=y, in_=acc[:])
                return
            acc_heads = acc[:].rearrange("p (h d) -> p h d", d=HEAD)
            y_heads = y.rearrange("p (h d) -> p h d", d=HEAD)
            nc.scalar.copy(out=y_heads[:, :, ROTATED:], in_=acc_heads[:, :, ROTATED:])
            acc_pairs = acc_heads[:, :, :ROTATED].rearrange("p h (i e) -> p h i e", e=2)
            y_pairs = y_heads[:, :, :ROTATED].rearrange("p h (i e) -> p h i e", e=2)
            plane_shape = [P, HEADS_IN_CHUNK, PAIRS]
            nc.vector.tensor_tensor(
                out=y_pairs,
                in0=acc_pairs,
                in1=trig[:, COS, t, :].unsqueeze(1).unsqueeze(3).to_broadcast(plane_shape + [2]),
                op=ALU.mult,
            )
            cross = cross_pool.tile([P, 2, HEADS_IN_CHUNK, PAIRS], F32)
            nc.vector.tensor_tensor(
                out=cross[:, 0],
                in0=acc_pairs[:, :, :, 1],
                in1=trig[:, NEG_SIN, t, :].unsqueeze(1).to_broadcast(plane_shape),
                op=ALU.mult,
            )
            nc.vector.tensor_tensor(
                out=cross[:, 1],
                in0=acc_pairs[:, :, :, 0],
                in1=trig[:, SIN, t, :].unsqueeze(1).to_broadcast(plane_shape),
                op=ALU.mult,
            )
            nc.gpsimd.tensor_tensor(
                out=y_pairs, in0=y_pairs, in1=cross[:].rearrange("p e h i -> p h i e"), op=ALU.add
            )

        for t in range(TOKEN_TILES):
            flip_and_quantise(t)
            keep_warm(WARM_BETWEEN[t])
        nc.scalar.activation(out=trig[:], in_=phase[:], func=ACT.Sin)

        for group in range(len(groups)):
            out_rows = groups[group][2]
            rotated = groups[group][3]
            width = out_rows.shape[1]
            ys = []
            for t in range(TOKEN_TILES):
                y = keep.tile([P, width], F32, name="y%d_%d" % (group, t))
                ys.append(y)
            for c in range(width // CHUNK):
                accs = []
                if group == 0:
                    for t in range(TOKEN_TILES):
                        acc = psum.tile([P, CHUNK], F32, tag="bank")
                        accs.append(acc)
                    for g in range(PASSES):
                        for t in range(TOKEN_TILES):
                            passes(accs[t], t, range(g, g + 1), group, c)
                elif group == len(groups) - 1:
                    for t in range(LAST_TILE):
                        acc = psum.tile([P, CHUNK], F32, tag="bank")
                        accs.append(acc)
                        passes(acc, t, range(PASSES), group, c)
                    for piece in LAST_PIECES:
                        acc = psum.tile([P, piece.stop - piece.start], F32, tag="bank")
                        accs.append(acc)
                        passes(acc, LAST_TILE, range(PASSES), group, c, piece)
                    for t in range(LAST_TILE):
                        empty_bank(accs[t], ys[t][:], t, rotated)
                        nc.sync.dma_start(out=out_rows[t * P : (t + 1) * P, :], in_=ys[t][:])
                    for i in range(len(LAST_PIECES)):
                        piece = LAST_PIECES[i]
                        empty_bank(accs[LAST_TILE + i], ys[LAST_TILE][:, piece], LAST_TILE, rotated)
                        nc.sync.dma_start(out=out_rows[LAST_TILE * P :, piece], in_=ys[LAST_TILE][:, piece])
                    continue
                else:
                    for t in range(TOKEN_TILES):
                        acc = psum.tile([P, CHUNK], F32, tag="bank")
                        accs.append(acc)
                        passes(acc, t, range(PASSES), group, c)
                for t in range(TOKEN_TILES):
                    empty_bank(accs[t], ys[t][:, c * CHUNK : (c + 1) * CHUNK], t, rotated)
                    if (c + 1) * CHUNK == width:
                        nc.sync.dma_start(out=out_rows[t * P : (t + 1) * P, :], in_=ys[t][:])
